import numpy as np
import ml_dtypes


def mxq(x, axis, fmt="e4m3"):
    dtype, down = {"e4m3": (ml_dtypes.float8_e4m3fn, 7), "e5m2": (ml_dtypes.float8_e5m2, 14)}[fmt]
    v = np.moveaxis(np.asarray(x, np.float32).astype(ml_dtypes.bfloat16).astype(np.float64), axis, -1)
    blocks = v.reshape(v.shape[:-1] + (-1, 32))
    amax = np.abs(blocks).max(-1, keepdims=True)
    byte = np.maximum(np.where(amax > 0, np.frexp(amax)[1] - 1 + 127, 0) - down, 1)
    scale = np.exp2(byte - 127.0)
    codes = (blocks / scale).astype(np.float32).astype(dtype).astype(np.float64)
    return np.moveaxis((codes * scale).reshape(v.shape), -1, axis)


WIDE = False


def mx_kscale(k):
    if not WIDE:
        return np.ones(k)
    levels = np.array([10, -10, 5, -5, 0])
    a = np.random.permutation(np.resize(levels, k // 512 * 4)).reshape(k // 512, 4)
    idx = np.arange(k)
    return np.exp2(a[idx // 512, idx % 128 // 32])


BF16 = ml_dtypes.bfloat16


def bf(x):
    return np.asarray(x, np.float32).astype(BF16)


def f64(x):
    return np.asarray(x).astype(np.float64)


E2M1 = np.array([0.0, 0.5, 1.0, 1.5, 2.0, 3.0, 4.0, 6.0, -0.0, -0.5, -1.0, -1.5, -2.0, -3.0, -4.0, -6.0])


def pack_weight(w, fmt):
    k, n = w.shape
    w = f64(bf(w)).reshape(k // 32, 32, n)
    amax = np.abs(w).max(1)
    if fmt == "e4m3":
        byte = np.frexp(amax)[1] - 1 + 127 - 7
    else:
        mant, ex = np.frexp(amax / 6.0)
        byte = np.where(mant > 0.5, ex, ex - 1) + 127
    byte = np.clip(np.where(amax > 0, byte, 1), 1, 254)
    scaled = (w * np.exp2(127.0 - byte)[:, None, :]).reshape(k, n).astype(np.float32)
    by_word = np.ascontiguousarray(scaled.reshape(k // 512, 128, 4, n).transpose(0, 1, 3, 2))
    if fmt == "e4m3":
        words = by_word.astype(ml_dtypes.float8_e4m3fn).view(np.uint8)
    else:
        c = by_word.astype(ml_dtypes.float4_e2m1fn).view(np.uint8) & 0xF
        words = c[..., 0::2] | (c[..., 1::2] << 4)
    return np.ascontiguousarray(words), np.ascontiguousarray(byte.astype(np.uint8).reshape(k // 512, 16, n))


def unpack_weight(words, scales, fmt):
    g, p, n, _ = words.shape
    if fmt == "e4m3":
        vals = np.ascontiguousarray(words).view(ml_dtypes.float8_e4m3fn).astype(np.float64)
    else:
        nib = np.empty((g, p, n, 4), np.uint8)
        nib[..., 0::2] = words & 0xF
        nib[..., 1::2] = words >> 4
        vals = E2M1[nib]
    vals = vals * np.repeat(np.exp2(scales.astype(np.float64) - 127.0), 8, axis=1)[..., None]
    return vals.transpose(0, 1, 3, 2).reshape(g * 512, n)

def pack4(w):
    words, scales = pack_weight(w, "e2m1")
    return words.reshape(words.shape[0], 128, -1), scales


def unpack4(words, scales):
    return unpack_weight(words.reshape(words.shape[0], 128, -1, 2), scales, "e2m1")


B, T, C, CO, HS, DW, DA, DV, DG = 8, 1024, 1024, 256, 64, 128, 128, 128, 256


def sigmoid(u):
    return 1.0 / (1.0 + np.exp(-u))


def setup_inputs():
    n = np.random.standard_normal
    s = mx_kscale(C)
    x = bf(n((B, T, C)) * s)
    x_v = bf(n((1, 1, C)) * 0.3)
    W_v_words, W_v_scales = pack4((n((CO, C)) / np.sqrt(C) / s).T)
    return {
        "x": x,
        "x_v": x_v,
        "W_v_words": W_v_words,
        "W_v_scales": W_v_scales,
        "v_hid": bf(n((B, T, DV))),
        "v2": bf(n((DV, CO)) / np.sqrt(DV)),
        "v0": bf(0.73 + n((1, 1, CO)) * 0.2),
        "v_first": bf(n((B, T, CO))),
    }


def reference(x, x_v, W_v_words, W_v_scales, v_hid, v2, v0, v_first):
    x = f64(x)
    prev = np.concatenate([np.zeros_like(x[:, :1]), x[:, :-1]], axis=1)
    xv = x + (prev - x) * f64(x_v)
    v = mxq(xv, 2, "e4m3") @ unpack4(W_v_words, W_v_scales)
    mix = sigmoid(f64(v0) + f64(v_hid) @ f64(v2))
    return v + (f64(v_first) - v) * mix

@@ -1,0 +1,341 @@
+from contextlib import ExitStack
+
+import concourse.mybir as mybir
+from concourse.masks import make_identity
+
+F32 = mybir.dt.float32
+BF16 = mybir.dt.bfloat16
+I32 = mybir.dt.int32
+U32 = mybir.dt.uint32
+U8 = mybir.dt.uint8
+FP8X4 = mybir.dt.float8_e4m3fn_x4
+FP4X4 = mybir.dt.float4_e2m1fn_x4
+ALU = mybir.AluOpType
+FUNC = mybir.ActivationFunctionType
+
+P = 128
+PACK = 4
+B, T, C, CO, DV = 8, 1024, 1024, 256, 128
+PASSES = C // (P * PACK)
+PLANES = PASSES * PACK
+BLOCK = 512
+TILES = BLOCK // P
+PAIR = 2
+PAD = 8
+RUN = 4
+BLOCKS = B * T // BLOCK
+BANKS = 2 * PASSES
+GPSIMD_TOKENS = 3 * P
+
+FLOPS = 2 * B * T * (C * CO + DV * CO)
+
+
+def tile_full_tmix_params_pb_t_kernel(
+    tc, x, x_v, W_v_words, W_v_scales, v_hid, v2, v0, v_first, out
+):
+    nc = tc.nc
+    with ExitStack() as pools:
+        const = pools.enter_context(tc.tile_pool(name="const", bufs=1))
+        pools.enter_context(tc.manual_schedule())
+        loads = pools.enter_context(tc.tile_pool(name="loads", bufs=3))
+        stage = pools.enter_context(tc.tile_pool(name="stage", bufs=2))
+        blend = pools.enter_context(tc.tile_pool(name="blend", bufs=3))
+        psum_x = pools.enter_context(tc.psum_pool(name="psum_x", bufs=4))
+        psum_h = pools.enter_context(tc.psum_pool(name="psum_h", bufs=1))
+        psum_z = pools.enter_context(tc.psum_pool(name="psum_z", bufs=1))
+        psum_v = pools.enter_context(tc.psum_pool(name="psum_v", bufs=2))
+
+        ident_f32 = const.tile([P, P], F32)
+        make_identity(nc, ident_f32[:])
+        ident_bf16 = const.tile([P, P], BF16)
+        make_identity(nc, ident_bf16[:])
+
+        xv_bf16 = const.tile([P, PASSES, PACK], BF16)
+        nc.sync.dma_start(
+            out=xv_bf16[:],
+            in_=x_v[0][0].rearrange("(g p t) -> p g t", g=PASSES, p=P, t=PACK),
+        )
+        w_prev = const.tile([P, PLANES], F32)
+        nc.vector.tensor_copy(out=w_prev[:], in_=xv_bf16[:].rearrange("p g t -> p (g t)"))
+        w_here = const.tile([P, PLANES], F32)
+        nc.vector.tensor_scalar(
+            out=w_here[:], in0=w_prev[:], scalar1=-1.0, scalar2=1.0, op0=ALU.mult, op1=ALU.add
+        )
+
+        w_words = const.tile([P, PASSES, 2 * CO], U8, align_bytes=64)
+        nc.sync.dma_start(
+            out=w_words[:].bitcast(I32),
+            in_=W_v_words.bitcast(I32).rearrange("g p n -> p g n"),
+        )
+        w_scales = const.tile([P, PASSES, CO], U8, align_bytes=64)
+        nc.vector.memset(w_scales[:].rearrange("p g n -> p (g n)").bitcast(I32), 0)
+        for quad in range(4):
+            nc.sync.dma_start(
+                out=w_scales[32 * quad : 32 * quad + 4, :, :].bitcast(I32),
+                in_=W_v_scales[:, 4 * quad : 4 * quad + 4, :]
+                .bitcast(I32)
+                .rearrange("g r n -> r g n"),
+            )
+
+        v2_sb = const.tile([P, CO], BF16)
+        nc.sync.dma_start(out=v2_sb[:], in_=v2)
+        v0_rows = const.tile([P, CO], BF16)
+        nc.sync.dma_start(out=v0_rows[:], in_=v0[0][0].partition_broadcast(P))
+        v0_rows_f32 = const.tile([P, CO], F32)
+        nc.vector.tensor_copy(out=v0_rows_f32[:], in_=v0_rows[:])
+        v0_ps = psum_z.tile([P, CO // P, P], F32, tag="z_ps")
+        for n in range(CO // P):
+            nc.tensor.transpose(v0_ps[:, n, :], v0_rows_f32[:, n * P : (n + 1) * P], ident_f32[:])
+        v0_cols = const.tile([P, CO // P, P], F32)
+        nc.vector.tensor_copy(out=v0_cols[:], in_=v0_ps[:])
+
+        shifted = [
+            const.tile([P, PLANES, PAD + T], F32, name="shifted_even"),
+            const.tile([P, PLANES, PAD + T], F32, name="shifted_odd"),
+        ]
+        for tile_ in shifted:
+            nc.vector.memset(tile_[:, :, 0:PAD], 0.0)
+
+        x_in, vh_in, vf_in = {}, {}, {}
+        turned, planes, grouped_in, codes_of, scales_of = {}, {}, {}, {}, {}
+        hidden_ps, hidden, z_acc, mix_of, v_acc, step_of = {}, {}, {}, {}, {}, {}
+
+        def live(block):
+            return 0 <= block < BLOCKS
+
+        def place(block):
+            return divmod(block * BLOCK, T)
+
+        def load(block):
+            if not live(block):
+                return
+            b, first = place(block)
+            tokens = slice(first, first + BLOCK)
+            x_in[block] = loads.tile([P, TILES, C], BF16, name="x_sb", bufs=3)
+            nc.sync.dma_start(
+                out=x_in[block][:], in_=x[b, tokens, :].rearrange("(j p) k -> p j k", p=P)
+            )
+            vh_in[block] = loads.tile([P, TILES, DV], BF16, name="vh_sb", bufs=3)
+            nc.sync.dma_start(
+                out=vh_in[block][:], in_=v_hid[b, tokens, :].rearrange("(j p) k -> p j k", p=P)
+            )
+            vf_in[block] = loads.tile([P, TILES, CO], BF16, name="vf_sb", bufs=5)
+            nc.sync.dma_start(
+                out=vf_in[block][:], in_=v_first[b, tokens, :].rearrange("(j p) n -> p j n", p=P)
+            )
+
+        def turn(block, bank):
+            if not live(block):
+                return
+            g, u = divmod(bank, 2)
+            xt = psum_x.tile([P, BLOCK], F32, name="xt")
+            for j in range(TILES):
+                words = x_in[block][:, j, :].bitcast(F32)
+                nc.tensor.transpose(
+                    xt[:, j * P : (j + 1) * P],
+                    words[:, 256 * g + u : 256 * (g + 1) : 2],
+                    ident_f32[:],
+                )
+            turned[(block, bank)] = xt
+
+        def scale_prev(block, bank):
+            if not live(block):
+                return
+            b, first = place(block)
+            halves = turned[(block, bank)][:].bitcast(BF16)
+            for e in range(2):
+                plane = 2 * bank + e
+                nc.scalar.activation(
+                    out=shifted[b % 2][:, plane, PAD + first : PAD + first + BLOCK],
+                    in_=halves[:, e : 2 * BLOCK : 2],
+                    func=FUNC.Copy,
+                    scale=w_prev[:, plane : plane + 1],
+                )
+
+        def mix_tokens(block, bank):
+            if not live(block):
+                return
+            b, first = place(block)
+            if bank == 0:
+                planes[block] = stage.tile([P, PLANES, BLOCK], BF16, name="xv_planes")
+            halves = turned[(block, bank)][:].bitcast(BF16)
+            for e in range(2):
+                plane = 2 * bank + e
+                nc.vector.scalar_tensor_tensor(
+                    out=planes[block][:, plane, :],
+                    in0=halves[:, e : 2 * BLOCK : 2],
+                    scalar=w_here[:, plane : plane + 1],
+                    in1=shifted[b % 2][:, plane, PAD - 1 + first : PAD - 1 + first + BLOCK],
+                    op0=ALU.mult,
+                    op1=ALU.add,
+                )
+
+        def regroup_on_gpsimd(block, g):
+            if not live(block):
+                return
+            if g == 0:
+                grouped_in[block] = stage.tile(
+                    [P, PASSES, BLOCK, PACK], BF16, name="grouped", align_bytes=64
+                )
+            nc.gpsimd.tensor_scalar(
+                out=grouped_in[block][:, g, 0:GPSIMD_TOKENS, :],
+                in0=planes[block][:, PACK * g : PACK * (g + 1), 0:GPSIMD_TOKENS].rearrange(
+                    "p t c -> p c t"
+                ),
+                scalar1=1.0,
+                scalar2=0.0,
+                op0=ALU.mult,
+                op1=ALU.add,
+            )
+
+        def regroup_on_scalar(block, g):
+            if not live(block):
+                return
+            nc.scalar.copy(
+                out=grouped_in[block][:, g, GPSIMD_TOKENS:BLOCK, :].rearrange(
+                    "p (c i) t -> p c t i", i=RUN
+                ),
+                in_=planes[block][:, PACK * g : PACK * (g + 1), GPSIMD_TOKENS:BLOCK].rearrange(
+                    "p t (c i) -> p c t i", i=RUN
+                ),
+            )
+
+        def quantise(block):
+            if not live(block):
+                return
+            codes_of[block] = stage.tile([P, PASSES * BLOCK], U32, name="codes", align_bytes=64)
+            scales_of[block] = stage.tile([P, PASSES * BLOCK], U8, name="scales", align_bytes=64)
+            nc.vector.quantize_mx(
+                out=codes_of[block][:].bitcast(FP8X4),
+                scales=scales_of[block][:],
+                in_=grouped_in[block][:].rearrange("p g c t -> p (g c t)"),
+            )
+
+        def project(block):
+            if not live(block):
+                return
+            for pair in range(TILES // PAIR):
+                v_ps = psum_v.tile([P, PAIR, CO], F32, name="v_ps")
+                for i in range(PAIR):
+                    j = pair * PAIR + i
+                    for n in range(CO // P):
+                        for g in range(PASSES):
+                            cols = slice(g * BLOCK + j * P, g * BLOCK + (j + 1) * P)
+                            nc.tensor.matmul_mx(
+                                out=v_ps[:, i, n * P : (n + 1) * P],
+                                lhsT=codes_of[block][:, cols].bitcast(FP8X4),
+                                lhsT_scale=scales_of[block][:, cols],
+                                rhs=w_words[:, g, 2 * P * n : 2 * P * (n + 1)].bitcast(FP4X4),
+                                rhs_scale=w_scales[:, g, n * P : (n + 1) * P],
+                                start=(g == 0),
+                                stop=(g == PASSES - 1),
+                            )
+                v_acc[(block, pair)] = v_ps
+
+        def turn_hidden(block):
+            if not live(block):
+                return
+            hidden_ps[block] = psum_h.tile([P, BLOCK], BF16, name="vht_ps")
+            for j in range(TILES):
+                nc.tensor.transpose(
+                    hidden_ps[block][:, j * P : (j + 1) * P], vh_in[block][:, j, :], ident_bf16[:]
+                )
+
+        def copy_hidden(block):
+            if not live(block):
+                return
+            hidden[block] = stage.tile([P, BLOCK], BF16, name="vht")
+            nc.scalar.copy(out=hidden[block][:], in_=hidden_ps[block][:])
+
+        def gate(block, pair):
+            if not live(block):
+                return
+            z_ps = psum_z.tile([P, PAIR, CO], F32, name="z_ps")
+            for i in range(PAIR):
+                j = pair * PAIR + i
+                for n in range(CO // P):
+                    nc.tensor.matmul(
+                        out=z_ps[:, i, n * P : (n + 1) * P],
+                        lhsT=v0_cols[:, n, :],
+                        rhs=ident_f32[:],
+                        is_transpose=True,
+                        start=(n == 0),
+                        stop=False,
+                    )
+                nc.tensor.matmul(
+                    out=z_ps[:, i, :],
+                    lhsT=hidden[block][:, j * P : (j + 1) * P],
+                    rhs=v2_sb[:],
+                    start=False,
+                    stop=True,
+                )
+            z_acc[(block, pair)] = z_ps
+
+        def squash(block, pair):
+            if not live(block):
+                return
+            mix_of[(block, pair)] = blend.tile([P, PAIR, CO], F32, name="mix", bufs=4)
+            nc.scalar.activation(
+                out=mix_of[(block, pair)][:], in_=z_acc[(block, pair)][:], func=FUNC.Sigmoid
+            )
+
+        def blend_start(block, pair):
+            if not live(block):
+                return
+            diff = blend.tile([P, PAIR, CO], F32, name="diff")
+            nc.vector.tensor_tensor(
+                out=diff[:],
+                in0=vf_in[block][:, pair * PAIR : (pair + 1) * PAIR, :],
+                in1=v_acc[(block, pair)][:],
+                op=ALU.subtract,
+            )
+            step_of[(block, pair)] = blend.tile([P, PAIR, CO], F32, name="step")
+            nc.gpsimd.tensor_tensor(
+                out=step_of[(block, pair)][:], in0=diff[:], in1=mix_of[(block, pair)][:], op=ALU.mult
+            )
+
+        def blend_finish(block, pair):
+            if not live(block):
+                return
+            b, first = place(block)
+            res = blend.tile([P, PAIR, CO], F32, name="res")
+            nc.vector.tensor_tensor(
+                out=res[:], in0=step_of[(block, pair)][:], in1=v_acc[(block, pair)][:], op=ALU.add
+            )
+            rows = slice(first + pair * PAIR * P, first + (pair + 1) * PAIR * P)
+            nc.sync.dma_start(out=out[b, rows, :].rearrange("(j p) n -> p j n", p=P), in_=res[:])
+
+        for i in range(-2, BLOCKS + 2):
+            load(i + 2)
+
+            scale_prev(i, 0)
+            squash(i - 1, 1)
+            mix_tokens(i, 0)
+            regroup_on_gpsimd(i - 1, 1)
+            blend_start(i - 2, 1)
+            turn(i, 3)
+            turn_hidden(i + 1)
+            gate(i, 0)
+            turn(i + 1, 0)
+
+            scale_prev(i, 1)
+            regroup_on_scalar(i - 1, 1)
+            mix_tokens(i, 1)
+            blend_finish(i - 2, 0)
+            regroup_on_gpsimd(i, 0)
+            turn(i + 1, 1)
+
+            scale_prev(i, 2)
+            copy_hidden(i + 1)
+            squash(i, 0)
+            mix_tokens(i, 2)
+            blend_finish(i - 2, 1)
+            quantise(i - 1)
+            project(i - 1)
+            gate(i, 1)
+
+            scale_prev(i, 3)
+            regroup_on_scalar(i, 0)
+            mix_tokens(i, 3)
+            blend_start(i - 1, 0)
+            turn(i + 1, 2)

@@ -308,34 +308,34 @@ def tile_full_tmix_params_pb_t_kernel(
         for i in range(-2, BLOCKS + 2):
             load(i + 2)
 
-            scale_prev(i, 0)
-            squash(i - 1, 1)
-            mix_tokens(i, 0)
-            regroup_on_gpsimd(i - 1, 1)
-            blend_start(i - 2, 1)
-            turn(i, 3)
-            turn_hidden(i + 1)
-            gate(i, 0)
-            turn(i + 1, 0)
-
             scale_prev(i, 1)
             regroup_on_scalar(i - 1, 1)
-            mix_tokens(i, 1)
-            blend_finish(i - 2, 0)
-            regroup_on_gpsimd(i, 0)
-            turn(i + 1, 1)
+            squash(i - 1, 0)
+            mix_tokens(i, 0)
+            regroup_on_gpsimd(i - 1, 1)
+            blend_start(i - 2, 0)
+            turn_hidden(i)
+            turn(i + 1, 0)
 
             scale_prev(i, 2)
-            copy_hidden(i + 1)
-            squash(i, 0)
-            mix_tokens(i, 2)
-            blend_finish(i - 2, 1)
-            quantise(i - 1)
-            project(i - 1)
-            gate(i, 1)
+            mix_tokens(i, 1)
+            blend_start(i - 2, 1)
+            gate(i - 1, 1)
+            turn(i + 1, 1)
 
             scale_prev(i, 3)
+            copy_hidden(i)
+            squash(i - 1, 1)
+            mix_tokens(i, 2)
+            blend_finish(i - 2, 0)
+            quantise(i - 1)
+            blend_finish(i - 2, 1)
+            regroup_on_gpsimd(i, 0)
+            turn(i + 1, 2)
+
+            scale_prev(i + 1, 0)
             regroup_on_scalar(i, 0)
             mix_tokens(i, 3)
-            blend_start(i - 1, 0)
-            turn(i + 1, 2)
+            gate(i, 0)
+            project(i - 1)
+            turn(i + 1, 3)

@@ -50,6 +50,17 @@ def tile_full_tmix_params_pb_t_kernel(
         ident_bf16 = const.tile([P, P], BF16)
         make_identity(nc, ident_bf16[:])
 
+        w_words = const.tile([P, PASSES, 2 * CO], U8, align_bytes=64)
+        w_scales = const.tile([P, PASSES, CO], U8, align_bytes=64)
+        nc.vector.memset(w_scales[:].rearrange("p g n -> p (g n)").bitcast(I32), 0)
+
+        shifted = [
+            const.tile([P, PLANES, PAD + T], F32, name="shifted_even"),
+            const.tile([P, PLANES, PAD + T], F32, name="shifted_odd"),
+        ]
+        for tile_ in shifted:
+            nc.vector.memset(tile_[:, :, 0:PAD], 0.0)
+
         xv_bf16 = const.tile([P, PASSES, PACK], BF16)
         nc.sync.dma_start(
             out=xv_bf16[:],
@@ -62,39 +73,15 @@ def tile_full_tmix_params_pb_t_kernel(
             out=w_here[:], in0=w_prev[:], scalar1=-1.0, scalar2=1.0, op0=ALU.mult, op1=ALU.add
         )
 
-        w_words = const.tile([P, PASSES, 2 * CO], U8, align_bytes=64)
-        nc.sync.dma_start(
-            out=w_words[:].bitcast(I32),
-            in_=W_v_words.bitcast(I32).rearrange("g p n -> p g n"),
-        )
-        w_scales = const.tile([P, PASSES, CO], U8, align_bytes=64)
-        nc.vector.memset(w_scales[:].rearrange("p g n -> p (g n)").bitcast(I32), 0)
-        for quad in range(4):
-            nc.sync.dma_start(
-                out=w_scales[32 * quad : 32 * quad + 4, :, :].bitcast(I32),
-                in_=W_v_scales[:, 4 * quad : 4 * quad + 4, :]
-                .bitcast(I32)
-                .rearrange("g r n -> r g n"),
-            )
-
         v2_sb = const.tile([P, CO], BF16)
         nc.sync.dma_start(out=v2_sb[:], in_=v2)
-        v0_rows = const.tile([P, CO], BF16)
-        nc.sync.dma_start(out=v0_rows[:], in_=v0[0][0].partition_broadcast(P))
-        v0_rows_f32 = const.tile([P, CO], F32)
-        nc.vector.tensor_copy(out=v0_rows_f32[:], in_=v0_rows[:])
-        v0_ps = psum_z.tile([P, CO // P, P], F32, tag="z_ps")
-        for n in range(CO // P):
-            nc.tensor.transpose(v0_ps[:, n, :], v0_rows_f32[:, n * P : (n + 1) * P], ident_f32[:])
+        v0_bf16 = const.tile([P, CO // P], BF16)
+        with nc.allow_non_contiguous_dma(reason="256 values, one to a partition and half"):
+            nc.sync.dma_start(out=v0_bf16[:], in_=v0[0][0].rearrange("(n c) -> c n", c=P))
         v0_cols = const.tile([P, CO // P, P], F32)
-        nc.vector.tensor_copy(out=v0_cols[:], in_=v0_ps[:])
-
-        shifted = [
-            const.tile([P, PLANES, PAD + T], F32, name="shifted_even"),
-            const.tile([P, PLANES, PAD + T], F32, name="shifted_odd"),
-        ]
-        for tile_ in shifted:
-            nc.vector.memset(tile_[:, :, 0:PAD], 0.0)
+        nc.vector.tensor_copy(
+            out=v0_cols[:], in_=v0_bf16[:].unsqueeze(2).to_broadcast([P, CO // P, P])
+        )
 
         x_in, vh_in, vf_in = {}, {}, {}
         turned, planes, grouped_in, codes_of, scales_of = {}, {}, {}, {}, {}
@@ -305,12 +292,23 @@ def tile_full_tmix_params_pb_t_kernel(
             rows = slice(first + pair * PAIR * P, first + (pair + 1) * PAIR * P)
             nc.sync.dma_start(out=out[b, rows, :].rearrange("(j p) n -> p j n", p=P), in_=res[:])
 
-        for i in range(-2, BLOCKS + 2):
+        load(0)
+        nc.sync.dma_start(
+            out=w_words[:].bitcast(I32), in_=W_v_words.bitcast(I32).rearrange("g p n -> p g n")
+        )
+        for quad in range(4):
+            nc.sync.dma_start(
+                out=w_scales[32 * quad : 32 * quad + 4, :, :].bitcast(I32),
+                in_=W_v_scales[:, 4 * quad : 4 * quad + 4, :]
+                .bitcast(I32)
+                .rearrange("g r n -> r g n"),
+            )
+
+        for i in range(-1, BLOCKS + 2):
             load(i + 2)
 
             scale_prev(i, 1)
             regroup_on_scalar(i - 1, 1)
-            squash(i - 1, 0)
             mix_tokens(i, 0)
             regroup_on_gpsimd(i - 1, 1)
             blend_start(i - 2, 0)
@@ -318,24 +316,25 @@ def tile_full_tmix_params_pb_t_kernel(
             turn(i + 1, 0)
 
             scale_prev(i, 2)
+            squash(i - 1, 0)
             mix_tokens(i, 1)
             blend_start(i - 2, 1)
-            gate(i - 1, 1)
             turn(i + 1, 1)
 
             scale_prev(i, 3)
             copy_hidden(i)
-            squash(i - 1, 1)
             mix_tokens(i, 2)
-            blend_finish(i - 2, 0)
             quantise(i - 1)
+            blend_finish(i - 2, 0)
             blend_finish(i - 2, 1)
             regroup_on_gpsimd(i, 0)
+            gate(i - 1, 1)
             turn(i + 1, 2)
 
             scale_prev(i + 1, 0)
             regroup_on_scalar(i, 0)
+            squash(i - 1, 1)
             mix_tokens(i, 3)
-            gate(i, 0)
             project(i - 1)
+            gate(i, 0)
             turn(i + 1, 3)

@@ -162,7 +162,7 @@ def tile_full_tmix_params_pb_t_kernel(
                 return
             if g == 0:
                 grouped_in[block] = stage.tile(
-                    [P, PASSES, BLOCK, PACK], BF16, name="grouped", align_bytes=64
+                    [P, PASSES, BLOCK, PACK], BF16, name="grouped", bufs=1, align_bytes=64
                 )
             nc.gpsimd.tensor_scalar(
                 out=grouped_in[block][:, g, 0:GPSIMD_TOKENS, :],

@@ -25,7 +25,7 @@ PAD = 8
 RUN = 4
 BLOCKS = B * T // BLOCK
 BANKS = 2 * PASSES
-GPSIMD_TOKENS = 3 * P
+GPSIMD_TOKENS = 5 * P // 2
 
 FLOPS = 2 * B * T * (C * CO + DV * CO)
 

@@ -312,13 +312,13 @@ def tile_full_tmix_params_pb_t_kernel(
             mix_tokens(i, 0)
             regroup_on_gpsimd(i - 1, 1)
             blend_start(i - 2, 0)
+            blend_start(i - 2, 1)
             turn_hidden(i)
             turn(i + 1, 0)
 
             scale_prev(i, 2)
             squash(i - 1, 0)
             mix_tokens(i, 1)
-            blend_start(i - 2, 1)
             turn(i + 1, 1)
 
             scale_prev(i, 3)

@@ -25,7 +25,7 @@ PAD = 8
 RUN = 4
 BLOCKS = B * T // BLOCK
 BANKS = 2 * PASSES
-GPSIMD_TOKENS = 5 * P // 2
+GPSIMD_TOKENS = (3 * P, 2 * P)
 
 FLOPS = 2 * B * T * (C * CO + DV * CO)
 
@@ -62,30 +62,19 @@ def tile_full_tmix_params_pb_t_kernel(
             nc.vector.memset(tile_[:, :, 0:PAD], 0.0)
 
         xv_bf16 = const.tile([P, PASSES, PACK], BF16)
-        nc.sync.dma_start(
-            out=xv_bf16[:],
-            in_=x_v[0][0].rearrange("(g p t) -> p g t", g=PASSES, p=P, t=PACK),
-        )
         w_prev = const.tile([P, PLANES], F32)
-        nc.vector.tensor_copy(out=w_prev[:], in_=xv_bf16[:].rearrange("p g t -> p (g t)"))
         w_here = const.tile([P, PLANES], F32)
-        nc.vector.tensor_scalar(
-            out=w_here[:], in0=w_prev[:], scalar1=-1.0, scalar2=1.0, op0=ALU.mult, op1=ALU.add
-        )
-
         v2_sb = const.tile([P, CO], BF16)
-        nc.sync.dma_start(out=v2_sb[:], in_=v2)
         v0_bf16 = const.tile([P, CO // P], BF16)
-        with nc.allow_non_contiguous_dma(reason="256 values, one to a partition and half"):
-            nc.sync.dma_start(out=v0_bf16[:], in_=v0[0][0].rearrange("(n c) -> c n", c=P))
         v0_cols = const.tile([P, CO // P, P], F32)
-        nc.vector.tensor_copy(
-            out=v0_cols[:], in_=v0_bf16[:].unsqueeze(2).to_broadcast([P, CO // P, P])
-        )
+
+        warm = const.tile([P, 2], F32)
+        nc.vector.memset(warm[:], 0.0)
+        nc.scalar.activation(out=warm[:, 1:2], in_=warm[:, 0:1], func=FUNC.Sigmoid)
 
         x_in, vh_in, vf_in = {}, {}, {}
         turned, planes, grouped_in, codes_of, scales_of = {}, {}, {}, {}, {}
-        hidden_ps, hidden, z_acc, mix_of, v_acc, step_of = {}, {}, {}, {}, {}, {}
+        hidden_ps, hidden, z_acc, mix_of, v_acc, diff_of, step_of = {}, {}, {}, {}, {}, {}, {}
 
         def live(block):
             return 0 <= block < BLOCKS
@@ -93,23 +82,37 @@ def tile_full_tmix_params_pb_t_kernel(
         def place(block):
             return divmod(block * BLOCK, T)
 
+        def load_x(block, g0, g1):
+            b, first = place(block)
+            cols = slice(g0 * P * PACK, g1 * P * PACK)
+            nc.sync.dma_start(
+                out=x_in[block][:, :, cols],
+                in_=x[b, first : first + BLOCK, cols].rearrange("(j p) k -> p j k", p=P),
+            )
+
+        def load_hidden(block):
+            b, first = place(block)
+            vh_in[block] = loads.tile([P, TILES, DV], BF16, name="vh_sb", bufs=3)
+            nc.sync.dma_start(
+                out=vh_in[block][:],
+                in_=v_hid[b, first : first + BLOCK, :].rearrange("(j p) k -> p j k", p=P),
+            )
+
+        def load_first(block):
+            b, first = place(block)
+            vf_in[block] = loads.tile([P, TILES, CO], BF16, name="vf_sb", bufs=5)
+            nc.sync.dma_start(
+                out=vf_in[block][:],
+                in_=v_first[b, first : first + BLOCK, :].rearrange("(j p) n -> p j n", p=P),
+            )
+
         def load(block):
             if not live(block):
                 return
-            b, first = place(block)
-            tokens = slice(first, first + BLOCK)
             x_in[block] = loads.tile([P, TILES, C], BF16, name="x_sb", bufs=3)
-            nc.sync.dma_start(
-                out=x_in[block][:], in_=x[b, tokens, :].rearrange("(j p) k -> p j k", p=P)
-            )
-            vh_in[block] = loads.tile([P, TILES, DV], BF16, name="vh_sb", bufs=3)
-            nc.sync.dma_start(
-                out=vh_in[block][:], in_=v_hid[b, tokens, :].rearrange("(j p) k -> p j k", p=P)
-            )
-            vf_in[block] = loads.tile([P, TILES, CO], BF16, name="vf_sb", bufs=5)
-            nc.sync.dma_start(
-                out=vf_in[block][:], in_=v_first[b, tokens, :].rearrange("(j p) n -> p j n", p=P)
-            )
+            load_x(block, 0, PASSES)
+            load_hidden(block)
+            load_first(block)
 
         def turn(block, bank):
             if not live(block):
@@ -165,8 +168,8 @@ def tile_full_tmix_params_pb_t_kernel(
                     [P, PASSES, BLOCK, PACK], BF16, name="grouped", bufs=1, align_bytes=64
                 )
             nc.gpsimd.tensor_scalar(
-                out=grouped_in[block][:, g, 0:GPSIMD_TOKENS, :],
-                in0=planes[block][:, PACK * g : PACK * (g + 1), 0:GPSIMD_TOKENS].rearrange(
+                out=grouped_in[block][:, g, 0 : GPSIMD_TOKENS[g], :],
+                in0=planes[block][:, PACK * g : PACK * (g + 1), 0 : GPSIMD_TOKENS[g]].rearrange(
                     "p t c -> p c t"
                 ),
                 scalar1=1.0,
@@ -179,10 +182,10 @@ def tile_full_tmix_params_pb_t_kernel(
             if not live(block):
                 return
             nc.scalar.copy(
-                out=grouped_in[block][:, g, GPSIMD_TOKENS:BLOCK, :].rearrange(
+                out=grouped_in[block][:, g, GPSIMD_TOKENS[g] : BLOCK, :].rearrange(
                     "p (c i) t -> p c t i", i=RUN
                 ),
-                in_=planes[block][:, PACK * g : PACK * (g + 1), GPSIMD_TOKENS:BLOCK].rearrange(
+                in_=planes[block][:, PACK * g : PACK * (g + 1), GPSIMD_TOKENS[g] : BLOCK].rearrange(
                     "p t (c i) -> p c t i", i=RUN
                 ),
             )
@@ -266,19 +269,26 @@ def tile_full_tmix_params_pb_t_kernel(
                 out=mix_of[(block, pair)][:], in_=z_acc[(block, pair)][:], func=FUNC.Sigmoid
             )
 
-        def blend_start(block, pair):
+        def difference(block, pair):
             if not live(block):
                 return
-            diff = blend.tile([P, PAIR, CO], F32, name="diff")
+            diff_of[(block, pair)] = blend.tile([P, PAIR, CO], F32, name="diff")
             nc.vector.tensor_tensor(
-                out=diff[:],
+                out=diff_of[(block, pair)][:],
                 in0=vf_in[block][:, pair * PAIR : (pair + 1) * PAIR, :],
                 in1=v_acc[(block, pair)][:],
                 op=ALU.subtract,
             )
+
+        def product(block, pair):
+            if not live(block):
+                return
             step_of[(block, pair)] = blend.tile([P, PAIR, CO], F32, name="step")
             nc.gpsimd.tensor_tensor(
-                out=step_of[(block, pair)][:], in0=diff[:], in1=mix_of[(block, pair)][:], op=ALU.mult
+                out=step_of[(block, pair)][:],
+                in0=diff_of[(block, pair)][:],
+                in1=mix_of[(block, pair)][:],
+                op=ALU.mult,
             )
 
         def blend_finish(block, pair):
@@ -292,7 +302,17 @@ def tile_full_tmix_params_pb_t_kernel(
             rows = slice(first + pair * PAIR * P, first + (pair + 1) * PAIR * P)
             nc.sync.dma_start(out=out[b, rows, :].rearrange("(j p) n -> p j n", p=P), in_=res[:])
 
-        load(0)
+        x_in[0] = loads.tile([P, TILES, C], BF16, name="x_sb", bufs=3)
+        load_x(0, 0, 1)
+        nc.sync.dma_start(
+            out=xv_bf16[:],
+            in_=x_v[0][0].rearrange("(g p t) -> p g t", g=PASSES, p=P, t=PACK),
+        )
+        load_x(0, 1, PASSES)
+        load_hidden(0)
+        nc.sync.dma_start(out=v2_sb[:], in_=v2)
+        with nc.allow_non_contiguous_dma(reason="256 values, one to a partition and half"):
+            nc.sync.dma_start(out=v0_bf16[:], in_=v0[0][0].rearrange("(n c) -> c n", c=P))
         nc.sync.dma_start(
             out=w_words[:].bitcast(I32), in_=W_v_words.bitcast(I32).rearrange("g p n -> p g n")
         )
@@ -303,16 +323,27 @@ def tile_full_tmix_params_pb_t_kernel(
                 .bitcast(I32)
                 .rearrange("g r n -> r g n"),
             )
+        load_first(0)
+
+        nc.vector.tensor_copy(out=w_prev[:], in_=xv_bf16[:].rearrange("p g t -> p (g t)"))
+        nc.vector.tensor_scalar(
+            out=w_here[:], in0=w_prev[:], scalar1=-1.0, scalar2=1.0, op0=ALU.mult, op1=ALU.add
+        )
+        nc.gpsimd.tensor_copy(
+            out=v0_cols[:], in_=v0_bf16[:].unsqueeze(2).to_broadcast([P, CO // P, P])
+        )
 
         for i in range(-1, BLOCKS + 2):
             load(i + 2)
 
             scale_prev(i, 1)
             regroup_on_scalar(i - 1, 1)
+            difference(i - 2, 0)
             mix_tokens(i, 0)
             regroup_on_gpsimd(i - 1, 1)
-            blend_start(i - 2, 0)
-            blend_start(i - 2, 1)
+            product(i - 2, 0)
+            difference(i - 2, 1)
+            product(i - 2, 1)
             turn_hidden(i)
             turn(i + 1, 0)
 

@@ -142,14 +142,14 @@ def tile_full_tmix_params_pb_t_kernel(
                     scale=w_prev[:, plane : plane + 1],
                 )
 
-        def mix_tokens(block, bank):
+        def mix_tokens(block, bank, which=(0, 1)):
             if not live(block):
                 return
             b, first = place(block)
-            if bank == 0:
+            if bank == 0 and 0 in which:
                 planes[block] = stage.tile([P, PLANES, BLOCK], BF16, name="xv_planes")
             halves = turned[(block, bank)][:].bitcast(BF16)
-            for e in range(2):
+            for e in which:
                 plane = 2 * bank + e
                 nc.vector.scalar_tensor_tensor(
                     out=planes[block][:, plane, :],
@@ -338,8 +338,9 @@ def tile_full_tmix_params_pb_t_kernel(
 
             scale_prev(i, 1)
             regroup_on_scalar(i - 1, 1)
+            mix_tokens(i, 0, (0,))
             difference(i - 2, 0)
-            mix_tokens(i, 0)
+            mix_tokens(i, 0, (1,))
             regroup_on_gpsimd(i - 1, 1)
             product(i - 2, 0)
             difference(i - 2, 1)

@@ -160,6 +160,9 @@ def tile_full_tmix_params_pb_t_kernel(
                     op1=ALU.add,
                 )
 
+        def gpsimd_tokens(block, g):
+            return BLOCK if PASSES * block + g < 3 else GPSIMD_TOKENS[g]
+
         def regroup_on_gpsimd(block, g):
             if not live(block):
                 return
@@ -168,8 +171,8 @@ def tile_full_tmix_params_pb_t_kernel(
                     [P, PASSES, BLOCK, PACK], BF16, name="grouped", bufs=1, align_bytes=64
                 )
             nc.gpsimd.tensor_scalar(
-                out=grouped_in[block][:, g, 0 : GPSIMD_TOKENS[g], :],
-                in0=planes[block][:, PACK * g : PACK * (g + 1), 0 : GPSIMD_TOKENS[g]].rearrange(
+                out=grouped_in[block][:, g, 0 : gpsimd_tokens(block, g), :],
+                in0=planes[block][:, PACK * g : PACK * (g + 1), 0 : gpsimd_tokens(block, g)].rearrange(
                     "p t c -> p c t"
                 ),
                 scalar1=1.0,
@@ -179,13 +182,13 @@ def tile_full_tmix_params_pb_t_kernel(
             )
 
         def regroup_on_scalar(block, g):
-            if not live(block):
+            if not live(block) or gpsimd_tokens(block, g) == BLOCK:
                 return
             nc.scalar.copy(
-                out=grouped_in[block][:, g, GPSIMD_TOKENS[g] : BLOCK, :].rearrange(
+                out=grouped_in[block][:, g, gpsimd_tokens(block, g) : BLOCK, :].rearrange(
                     "p (c i) t -> p c t i", i=RUN
                 ),
-                in_=planes[block][:, PACK * g : PACK * (g + 1), GPSIMD_TOKENS[g] : BLOCK].rearrange(
+                in_=planes[block][:, PACK * g : PACK * (g + 1), gpsimd_tokens(block, g) : BLOCK].rearrange(
                     "p t (c i) -> p c t i", i=RUN
                 ),
             )

@@ -62,6 +62,10 @@ def tile_full_tmix_params_pb_t_kernel(
             nc.vector.memset(tile_[:, :, 0:PAD], 0.0)
 
         xv_bf16 = const.tile([P, PASSES, PACK], BF16)
+        nc.scalar.dma_start(
+            out=xv_bf16[:],
+            in_=x_v[0][0].rearrange("(g p t) -> p g t", g=PASSES, p=P, t=PACK),
+        )
         w_prev = const.tile([P, PLANES], F32)
         w_here = const.tile([P, PLANES], F32)
         v2_sb = const.tile([P, CO], BF16)
@@ -82,13 +86,15 @@ def tile_full_tmix_params_pb_t_kernel(
         def place(block):
             return divmod(block * BLOCK, T)
 
-        def load_x(block, g0, g1):
+        def load_x(block, g0, g1, tiles=TILES):
             b, first = place(block)
             cols = slice(g0 * P * PACK, g1 * P * PACK)
-            nc.sync.dma_start(
-                out=x_in[block][:, :, cols],
-                in_=x[b, first : first + BLOCK, cols].rearrange("(j p) k -> p j k", p=P),
-            )
+            for j in range(0, TILES, tiles):
+                rows = slice(first + j * P, first + (j + tiles) * P)
+                nc.sync.dma_start(
+                    out=x_in[block][:, j : j + tiles, cols],
+                    in_=x[b, rows, cols].rearrange("(j p) k -> p j k", p=P),
+                )
 
         def load_hidden(block):
             b, first = place(block)
@@ -181,17 +187,19 @@ def tile_full_tmix_params_pb_t_kernel(
                 op1=ALU.add,
             )
 
-        def regroup_on_scalar(block, g):
-            if not live(block) or gpsimd_tokens(block, g) == BLOCK:
-                return
-            nc.scalar.copy(
-                out=grouped_in[block][:, g, gpsimd_tokens(block, g) : BLOCK, :].rearrange(
-                    "p (c i) t -> p c t i", i=RUN
-                ),
-                in_=planes[block][:, PACK * g : PACK * (g + 1), gpsimd_tokens(block, g) : BLOCK].rearrange(
+        def regroup_views(block, g, c0, c1):
+            return (
+                grouped_in[block][:, g, c0:c1, :].rearrange("p (c i) t -> p c t i", i=RUN),
+                planes[block][:, PACK * g : PACK * (g + 1), c0:c1].rearrange(
                     "p t (c i) -> p c t i", i=RUN
                 ),
             )
+
+        def regroup_on_scalar(block, g):
+            if not live(block) or gpsimd_tokens(block, g) == BLOCK:
+                return
+            grouped, flat = regroup_views(block, g, gpsimd_tokens(block, g), BLOCK)
+            nc.scalar.copy(out=grouped, in_=flat)
 
         def quantise(block):
             if not live(block):
@@ -208,7 +216,10 @@ def tile_full_tmix_params_pb_t_kernel(
             if not live(block):
                 return
             for pair in range(TILES // PAIR):
-                v_ps = psum_v.tile([P, PAIR, CO], F32, name="v_ps")
+                if block == BLOCKS - 1:
+                    v_ps = psum_x.tile([P, PAIR, CO], F32, name="xt")
+                else:
+                    v_ps = psum_v.tile([P, PAIR, CO], F32, name="v_ps")
                 for i in range(PAIR):
                     j = pair * PAIR + i
                     for n in range(CO // P):
@@ -283,11 +294,11 @@ def tile_full_tmix_params_pb_t_kernel(
                 op=ALU.subtract,
             )
 
-        def product(block, pair):
+        def product(block, pair, engine=nc.gpsimd):
             if not live(block):
                 return
             step_of[(block, pair)] = blend.tile([P, PAIR, CO], F32, name="step")
-            nc.gpsimd.tensor_tensor(
+            engine.tensor_tensor(
                 out=step_of[(block, pair)][:],
                 in0=diff_of[(block, pair)][:],
                 in1=mix_of[(block, pair)][:],
@@ -306,11 +317,7 @@ def tile_full_tmix_params_pb_t_kernel(
             nc.sync.dma_start(out=out[b, rows, :].rearrange("(j p) n -> p j n", p=P), in_=res[:])
 
         x_in[0] = loads.tile([P, TILES, C], BF16, name="x_sb", bufs=3)
-        load_x(0, 0, 1)
-        nc.sync.dma_start(
-            out=xv_bf16[:],
-            in_=x_v[0][0].rearrange("(g p t) -> p g t", g=PASSES, p=P, t=PACK),
-        )
+        load_x(0, 0, 1, tiles=1)
         load_x(0, 1, PASSES)
         load_hidden(0)
         nc.sync.dma_start(out=v2_sb[:], in_=v2)
@@ -336,7 +343,7 @@ def tile_full_tmix_params_pb_t_kernel(
             out=v0_cols[:], in_=v0_bf16[:].unsqueeze(2).to_broadcast([P, CO // P, P])
         )
 
-        for i in range(-1, BLOCKS + 2):
+        for i in range(-1, BLOCKS - 1):
             load(i + 2)
 
             scale_prev(i, 1)
@@ -373,3 +380,56 @@ def tile_full_tmix_params_pb_t_kernel(
             project(i - 1)
             gate(i, 0)
             turn(i + 1, 3)
+
+        last = BLOCKS - 1
+        scale_prev(last, 1)
+        regroup_on_scalar(last - 1, 1)
+        mix_tokens(last, 0, (0,))
+        difference(last - 2, 0)
+        mix_tokens(last, 0, (1,))
+        regroup_on_gpsimd(last - 1, 1)
+        product(last - 2, 0)
+        difference(last - 2, 1)
+        product(last - 2, 1)
+        turn_hidden(last)
+
+        scale_prev(last, 2)
+        squash(last - 1, 0)
+        mix_tokens(last, 1)
+
+        scale_prev(last, 3)
+        copy_hidden(last)
+        mix_tokens(last, 2)
+        quantise(last - 1)
+        blend_finish(last - 2, 0)
+        blend_finish(last - 2, 1)
+        regroup_on_gpsimd(last, 0)
+        gate(last - 1, 1)
+
+        squash(last - 1, 1)
+        regroup_on_scalar(last, 0)
+        mix_tokens(last, 3)
+        gate(last, 0)
+        project(last - 1)
+        squash(last, 0)
+        gate(last, 1)
+
+        difference(last - 1, 0)
+        grouped, flat = regroup_views(last, PASSES - 1, 0, BLOCK // 2)
+        nc.vector.tensor_copy(out=grouped, in_=flat)
+        grouped, flat = regroup_views(last, PASSES - 1, BLOCK // 2, BLOCK)
+        nc.scalar.copy(out=grouped, in_=flat)
+        squash(last, 1)
+        quantise(last)
+        project(last)
+        difference(last - 1, 1)
+        product(last - 1, 0, nc.vector)
+        product(last - 1, 1)
+        blend_finish(last - 1, 0)
+        difference(last, 0)
+        blend_finish(last - 1, 1)
+        difference(last, 1)
+        product(last, 0)
+        product(last, 1, nc.vector)
+        blend_finish(last, 0)
+        blend_finish(last, 1)

@@ -86,15 +86,21 @@ def tile_full_tmix_params_pb_t_kernel(
         def place(block):
             return divmod(block * BLOCK, T)
 
-        def load_x(block, g0, g1, tiles=TILES):
+        def load_x(block, x_tile, g0, g1, tiles=TILES):
             b, first = place(block)
             cols = slice(g0 * P * PACK, g1 * P * PACK)
             for j in range(0, TILES, tiles):
                 rows = slice(first + j * P, first + (j + tiles) * P)
                 nc.sync.dma_start(
-                    out=x_in[block][:, j : j + tiles, cols],
+                    out=x_tile[:, j : j + tiles, :],
                     in_=x[b, rows, cols].rearrange("(j p) k -> p j k", p=P),
                 )
+            for g in range(g0, g1):
+                x_in[(block, g)] = x_tile[:, :, (g - g0) * P * PACK : (g - g0 + 1) * P * PACK]
+
+        def load_x_block(block):
+            x_tile = loads.tile([P, TILES, C], BF16, name="x_sb", bufs=3)
+            load_x(block, x_tile, 0, PASSES)
 
         def load_hidden(block):
             b, first = place(block)
@@ -115,56 +121,58 @@ def tile_full_tmix_params_pb_t_kernel(
         def load(block):
             if not live(block):
                 return
-            x_in[block] = loads.tile([P, TILES, C], BF16, name="x_sb", bufs=3)
-            load_x(block, 0, PASSES)
+            load_x_block(block)
             load_hidden(block)
             load_first(block)
+
+        def turn_part(block, bank, j0, j1, pool, name):
+            g, u = divmod(bank, 2)
+            xt = pool.tile([P, (j1 - j0) * P], F32, name=name)
+            for j in range(j0, j1):
+                words = x_in[(block, g)][:, j, :].bitcast(F32)
+                nc.tensor.transpose(
+                    xt[:, (j - j0) * P : (j - j0 + 1) * P], words[:, u::2], ident_f32[:]
+                )
+            turned.setdefault((block, bank), []).append((xt, j0 * P, j1 * P))
 
         def turn(block, bank):
             if not live(block):
                 return
-            g, u = divmod(bank, 2)
-            xt = psum_x.tile([P, BLOCK], F32, name="xt")
-            for j in range(TILES):
-                words = x_in[block][:, j, :].bitcast(F32)
-                nc.tensor.transpose(
-                    xt[:, j * P : (j + 1) * P],
-                    words[:, 256 * g + u : 256 * (g + 1) : 2],
-                    ident_f32[:],
-                )
-            turned[(block, bank)] = xt
+            turn_part(block, bank, 0, TILES, psum_x, "xt")
 
         def scale_prev(block, bank):
             if not live(block):
                 return
             b, first = place(block)
-            halves = turned[(block, bank)][:].bitcast(BF16)
-            for e in range(2):
-                plane = 2 * bank + e
-                nc.scalar.activation(
-                    out=shifted[b % 2][:, plane, PAD + first : PAD + first + BLOCK],
-                    in_=halves[:, e : 2 * BLOCK : 2],
-                    func=FUNC.Copy,
-                    scale=w_prev[:, plane : plane + 1],
-                )
+            for xt, c0, c1 in turned[(block, bank)]:
+                halves = xt[:].bitcast(BF16)
+                for e in range(2):
+                    plane = 2 * bank + e
+                    nc.scalar.activation(
+                        out=shifted[b % 2][:, plane, PAD + first + c0 : PAD + first + c1],
+                        in_=halves[:, e : 2 * (c1 - c0) : 2],
+                        func=FUNC.Copy,
+                        scale=w_prev[:, plane : plane + 1],
+                    )
 
         def mix_tokens(block, bank, which=(0, 1)):
             if not live(block):
                 return
             b, first = place(block)
-            if bank == 0 and 0 in which:
+            if block not in planes:
                 planes[block] = stage.tile([P, PLANES, BLOCK], BF16, name="xv_planes")
-            halves = turned[(block, bank)][:].bitcast(BF16)
-            for e in which:
-                plane = 2 * bank + e
-                nc.vector.scalar_tensor_tensor(
-                    out=planes[block][:, plane, :],
-                    in0=halves[:, e : 2 * BLOCK : 2],
-                    scalar=w_here[:, plane : plane + 1],
-                    in1=shifted[b % 2][:, plane, PAD - 1 + first : PAD - 1 + first + BLOCK],
-                    op0=ALU.mult,
-                    op1=ALU.add,
-                )
+            for xt, c0, c1 in turned[(block, bank)]:
+                halves = xt[:].bitcast(BF16)
+                for e in which:
+                    plane = 2 * bank + e
+                    nc.vector.scalar_tensor_tensor(
+                        out=planes[block][:, plane, c0:c1],
+                        in0=halves[:, e : 2 * (c1 - c0) : 2],
+                        scalar=w_here[:, plane : plane + 1],
+                        in1=shifted[b % 2][:, plane, PAD - 1 + first + c0 : PAD - 1 + first + c1],
+                        op0=ALU.mult,
+                        op1=ALU.add,
+                    )
 
         def gpsimd_tokens(block, g):
             return BLOCK if PASSES * block + g < 3 else GPSIMD_TOKENS[g]
@@ -316,10 +324,11 @@ def tile_full_tmix_params_pb_t_kernel(
             rows = slice(first + pair * PAIR * P, first + (pair + 1) * PAIR * P)
             nc.sync.dma_start(out=out[b, rows, :].rearrange("(j p) n -> p j n", p=P), in_=res[:])
 
-        x_in[0] = loads.tile([P, TILES, C], BF16, name="x_sb", bufs=3)
-        load_x(0, 0, 1, tiles=1)
-        load_x(0, 1, PASSES)
+        for g in range(PASSES):
+            x_pass = const.tile([P, TILES, P * PACK], BF16, name="x_pass%d" % g)
+            load_x(0, x_pass, g, g + 1, tiles=1 if g == 0 else TILES)
         load_hidden(0)
+        load_x_block(1)
         nc.sync.dma_start(out=v2_sb[:], in_=v2)
         with nc.allow_non_contiguous_dma(reason="256 values, one to a partition and half"):
             nc.sync.dma_start(out=v0_bf16[:], in_=v0[0][0].rearrange("(n c) -> c n", c=P))
@@ -343,7 +352,19 @@ def tile_full_tmix_params_pb_t_kernel(
             out=v0_cols[:], in_=v0_bf16[:].unsqueeze(2).to_broadcast([P, CO // P, P])
         )
 
-        for i in range(-1, BLOCKS - 1):
+        load_hidden(1)
+        load_first(1)
+        turn_part(0, 0, 0, 1, psum_v, "v_ps")
+        turn_part(0, 0, 1, 2, psum_v, "v_ps")
+        turn_part(0, 0, 2, TILES, psum_x, "xt")
+        turn(0, 1)
+        turn(0, 2)
+        scale_prev(0, 0)
+        turn(0, 3)
+        mix_tokens(0, 0)
+        turned[(0, 0)] = []
+
+        for i in range(BLOCKS - 1):
             load(i + 2)
 
             scale_prev(i, 1)

@@ -79,6 +79,7 @@ def tile_full_tmix_params_pb_t_kernel(
         x_in, vh_in, vf_in = {}, {}, {}
         turned, planes, grouped_in, codes_of, scales_of = {}, {}, {}, {}, {}
         hidden_ps, hidden, z_acc, mix_of, v_acc, diff_of, step_of = {}, {}, {}, {}, {}, {}, {}
+        result = {}
 
         def live(block):
             return 0 <= block < BLOCKS
@@ -99,10 +100,14 @@ def tile_full_tmix_params_pb_t_kernel(
                 x_in[(block, g)] = x_tile[:, :, (g - g0) * P * PACK : (g - g0 + 1) * P * PACK]
 
         def load_x_block(block):
-            x_tile = loads.tile([P, TILES, C], BF16, name="x_sb", bufs=3)
+            if not live(block):
+                return
+            x_tile = loads.tile([P, TILES, C], BF16, name="x_sb", bufs=4)
             load_x(block, x_tile, 0, PASSES)
 
         def load_hidden(block):
+            if not live(block):
+                return
             b, first = place(block)
             vh_in[block] = loads.tile([P, TILES, DV], BF16, name="vh_sb", bufs=3)
             nc.sync.dma_start(
@@ -112,18 +117,10 @@ def tile_full_tmix_params_pb_t_kernel(
 
         def load_first(block):
             b, first = place(block)
-            vf_in[block] = loads.tile([P, TILES, CO], BF16, name="vf_sb", bufs=5)
-            nc.sync.dma_start(
-                out=vf_in[block][:],
-                in_=v_first[b, first : first + BLOCK, :].rearrange("(j p) n -> p j n", p=P),
-            )
-
-        def load(block):
-            if not live(block):
+            if not live(block) or first > 0:
                 return
-            load_x_block(block)
-            load_hidden(block)
-            load_first(block)
+            vf_in[b] = loads.tile([P, T // P, CO], BF16, name="vf_sb", bufs=3)
+            nc.sync.dma_start(out=vf_in[b][:], in_=v_first[b].rearrange("(j p) n -> p j n", p=P))
 
         def turn_part(block, bank, j0, j1, pool, name):
             g, u = divmod(bank, 2)
@@ -160,7 +157,7 @@ def tile_full_tmix_params_pb_t_kernel(
                 return
             b, first = place(block)
             if block not in planes:
-                planes[block] = stage.tile([P, PLANES, BLOCK], BF16, name="xv_planes")
+                planes[block] = stage.tile([P, PLANES, BLOCK], BF16, name="xv_planes", bufs=3)
             for xt, c0, c1 in turned[(block, bank)]:
                 halves = xt[:].bitcast(BF16)
                 for e in which:
@@ -212,8 +209,8 @@ def tile_full_tmix_params_pb_t_kernel(
         def quantise(block):
             if not live(block):
                 return
-            codes_of[block] = stage.tile([P, PASSES * BLOCK], U32, name="codes", align_bytes=64)
-            scales_of[block] = stage.tile([P, PASSES * BLOCK], U8, name="scales", align_bytes=64)
+            codes_of[block] = stage.tile([P, PASSES * BLOCK], U32, name="codes", bufs=3, align_bytes=64)
+            scales_of[block] = stage.tile([P, PASSES * BLOCK], U8, name="scales", bufs=3, align_bytes=64)
             nc.vector.quantize_mx(
                 out=codes_of[block][:].bitcast(FP8X4),
                 scales=scales_of[block][:],
@@ -294,10 +291,12 @@ def tile_full_tmix_params_pb_t_kernel(
         def difference(block, pair):
             if not live(block):
                 return
+            b, first = place(block)
+            j = first // P + pair * PAIR
             diff_of[(block, pair)] = blend.tile([P, PAIR, CO], F32, name="diff")
             nc.vector.tensor_tensor(
                 out=diff_of[(block, pair)][:],
-                in0=vf_in[block][:, pair * PAIR : (pair + 1) * PAIR, :],
+                in0=vf_in[b][:, j : j + PAIR, :],
                 in1=v_acc[(block, pair)][:],
                 op=ALU.subtract,
             )
@@ -317,12 +316,26 @@ def tile_full_tmix_params_pb_t_kernel(
             if not live(block):
                 return
             b, first = place(block)
-            res = blend.tile([P, PAIR, CO], F32, name="res")
+            if pair == 0:
+                result[block] = blend.tile([P, TILES, CO], F32, name="res", bufs=10)
+            tiles = slice(pair * PAIR, (pair + 1) * PAIR)
             nc.vector.tensor_tensor(
-                out=res[:], in0=step_of[(block, pair)][:], in1=v_acc[(block, pair)][:], op=ALU.add
+                out=result[block][:, tiles, :],
+                in0=step_of[(block, pair)][:],
+                in1=v_acc[(block, pair)][:],
+                op=ALU.add,
             )
-            rows = slice(first + pair * PAIR * P, first + (pair + 1) * PAIR * P)
-            nc.sync.dma_start(out=out[b, rows, :].rearrange("(j p) n -> p j n", p=P), in_=res[:])
+            if block == BLOCKS - 1:
+                store(block, tiles)
+            elif pair == TILES // PAIR - 1:
+                store(block, slice(0, TILES))
+
+        def store(block, tiles):
+            b, first = place(block)
+            rows = slice(first + tiles.start * P, first + tiles.stop * P)
+            nc.sync.dma_start(
+                out=out[b, rows, :].rearrange("(j p) n -> p j n", p=P), in_=result[block][:, tiles, :]
+            )
 
         for g in range(PASSES):
             x_pass = const.tile([P, TILES, P * PACK], BF16, name="x_pass%d" % g)
@@ -332,6 +345,8 @@ def tile_full_tmix_params_pb_t_kernel(
         nc.sync.dma_start(out=v2_sb[:], in_=v2)
         with nc.allow_non_contiguous_dma(reason="256 values, one to a partition and half"):
             nc.sync.dma_start(out=v0_bf16[:], in_=v0[0][0].rearrange("(n c) -> c n", c=P))
+        load_hidden(1)
+        load_x_block(2)
         nc.sync.dma_start(
             out=w_words[:].bitcast(I32), in_=W_v_words.bitcast(I32).rearrange("g p n -> p g n")
         )
@@ -352,8 +367,6 @@ def tile_full_tmix_params_pb_t_kernel(
             out=v0_cols[:], in_=v0_bf16[:].unsqueeze(2).to_broadcast([P, CO // P, P])
         )
 
-        load_hidden(1)
-        load_first(1)
         turn_part(0, 0, 0, 1, psum_v, "v_ps")
         turn_part(0, 0, 1, 2, psum_v, "v_ps")
         turn_part(0, 0, 2, TILES, psum_x, "xt")
@@ -365,7 +378,9 @@ def tile_full_tmix_params_pb_t_kernel(
         turned[(0, 0)] = []
 
         for i in range(BLOCKS - 1):
-            load(i + 2)
+            load_x_block(i + 3)
+            load_hidden(i + 2)
+            load_first(i + 2)
 
             scale_prev(i, 1)
             regroup_on_scalar(i - 1, 1)

@@ -21,7 +21,8 @@ PLANES = PASSES * PACK
 BLOCK = 512
 TILES = BLOCK // P
 PAIR = 2
-PAD = 8
+PAD = 9
+ROW = PAD + T + 7
 RUN = 4
 BLOCKS = B * T // BLOCK
 BANKS = 2 * PASSES
@@ -55,8 +56,8 @@ def tile_full_tmix_params_pb_t_kernel(
         nc.vector.memset(w_scales[:].rearrange("p g n -> p (g n)").bitcast(I32), 0)
 
         shifted = [
-            const.tile([P, PLANES, PAD + T], F32, name="shifted_even"),
-            const.tile([P, PLANES, PAD + T], F32, name="shifted_odd"),
+            const.tile([P, PLANES, ROW], F32, name="shifted_even"),
+            const.tile([P, PLANES, ROW], F32, name="shifted_odd"),
         ]
         for tile_ in shifted:
             nc.vector.memset(tile_[:, :, 0:PAD], 0.0)
@@ -172,7 +173,7 @@ def tile_full_tmix_params_pb_t_kernel(
                     )
 
         def gpsimd_tokens(block, g):
-            return BLOCK if PASSES * block + g < 3 else GPSIMD_TOKENS[g]
+            return BLOCK if block == 0 else GPSIMD_TOKENS[g]
 
         def regroup_on_gpsimd(block, g):
             if not live(block):

@@ -26,7 +26,7 @@ ROW = PAD + T + 7
 RUN = 4
 BLOCKS = B * T // BLOCK
 BANKS = 2 * PASSES
-GPSIMD_TOKENS = (3 * P, 2 * P)
+GPSIMD_TOKENS = (3 * P, 7 * P // 4)
 
 FLOPS = 2 * B * T * (C * CO + DV * CO)
 

@@ -77,6 +77,9 @@ def tile_full_tmix_params_pb_t_kernel(
         nc.vector.memset(warm[:], 0.0)
         nc.scalar.activation(out=warm[:, 1:2], in_=warm[:, 0:1], func=FUNC.Sigmoid)
 
+        with nc.allow_non_contiguous_dma(reason="256 values, one to a partition and half"):
+            nc.scalar.dma_start(out=v0_bf16[:], in_=v0[0][0].rearrange("(n c) -> c n", c=P))
+
         x_in, vh_in, vf_in = {}, {}, {}
         turned, planes, grouped_in, codes_of, scales_of = {}, {}, {}, {}, {}
         hidden_ps, hidden, z_acc, mix_of, v_acc, diff_of, step_of = {}, {}, {}, {}, {}, {}, {}
@@ -344,8 +347,6 @@ def tile_full_tmix_params_pb_t_kernel(
         load_hidden(0)
         load_x_block(1)
         nc.sync.dma_start(out=v2_sb[:], in_=v2)
-        with nc.allow_non_contiguous_dma(reason="256 values, one to a partition and half"):
-            nc.sync.dma_start(out=v0_bf16[:], in_=v0[0][0].rearrange("(n c) -> c n", c=P))
         load_hidden(1)
         load_x_block(2)
         nc.sync.dma_start(

@@ -27,6 +27,7 @@ RUN = 4
 BLOCKS = B * T // BLOCK
 BANKS = 2 * PASSES
 GPSIMD_TOKENS = (3 * P, 7 * P // 4)
+LAST_GPSIMD_TOKENS = 3 * P // 2
 
 FLOPS = 2 * B * T * (C * CO + DV * CO)
 
@@ -452,15 +453,21 @@ def tile_full_tmix_params_pb_t_kernel(
         squash(last, 0)
         gate(last, 1)
 
-        difference(last - 1, 0)
-        grouped, flat = regroup_views(last, PASSES - 1, 0, BLOCK // 2)
-        nc.vector.tensor_copy(out=grouped, in_=flat)
-        grouped, flat = regroup_views(last, PASSES - 1, BLOCK // 2, BLOCK)
+        grouped, flat = regroup_views(last, PASSES - 1, LAST_GPSIMD_TOKENS, BLOCK)
         nc.scalar.copy(out=grouped, in_=flat)
+        nc.gpsimd.tensor_scalar(
+            out=grouped_in[last][:, PASSES - 1, 0:LAST_GPSIMD_TOKENS, :],
+            in0=planes[last][:, PACK * (PASSES - 1) :, 0:LAST_GPSIMD_TOKENS].rearrange("p t c -> p c t"),
+            scalar1=1.0,
+            scalar2=0.0,
+            op0=ALU.mult,
+            op1=ALU.add,
+        )
+        difference(last - 1, 0)
+        difference(last - 1, 1)
         squash(last, 1)
         quantise(last)
         project(last)
-        difference(last - 1, 1)
         product(last - 1, 0, nc.vector)
         product(last - 1, 1)
         blend_finish(last - 1, 0)

from contextlib import ExitStack

import concourse.mybir as mybir
from concourse.masks import make_identity

F32 = mybir.dt.float32
BF16 = mybir.dt.bfloat16
I32 = mybir.dt.int32
U32 = mybir.dt.uint32
U8 = mybir.dt.uint8
FP8X4 = mybir.dt.float8_e4m3fn_x4
FP4X4 = mybir.dt.float4_e2m1fn_x4
ALU = mybir.AluOpType
FUNC = mybir.ActivationFunctionType

P = 128
PACK = 4
B, T, C, CO, DV = 8, 1024, 1024, 256, 128
PASSES = C // (P * PACK)
PLANES = PASSES * PACK
BLOCK = 512
TILES = BLOCK // P
PAIR = 2
PAD = 9
ROW = PAD + T + 7
RUN = 4
BLOCKS = B * T // BLOCK
BANKS = 2 * PASSES
GPSIMD_TOKENS = (3 * P, 7 * P // 4)
LAST_GPSIMD_TOKENS = 3 * P // 2

FLOPS = 2 * B * T * (C * CO + DV * CO)


def tile_full_tmix_params_pb_t_kernel(
    tc, x, x_v, W_v_words, W_v_scales, v_hid, v2, v0, v_first, out
):
    nc = tc.nc
    with ExitStack() as pools:
        const = pools.enter_context(tc.tile_pool(name="const", bufs=1))
        pools.enter_context(tc.manual_schedule())
        loads = pools.enter_context(tc.tile_pool(name="loads", bufs=3))
        stage = pools.enter_context(tc.tile_pool(name="stage", bufs=2))
        blend = pools.enter_context(tc.tile_pool(name="blend", bufs=3))
        psum_x = pools.enter_context(tc.psum_pool(name="psum_x", bufs=4))
        psum_h = pools.enter_context(tc.psum_pool(name="psum_h", bufs=1))
        psum_z = pools.enter_context(tc.psum_pool(name="psum_z", bufs=1))
        psum_v = pools.enter_context(tc.psum_pool(name="psum_v", bufs=2))

        ident_f32 = const.tile([P, P], F32)
        make_identity(nc, ident_f32[:])
        ident_bf16 = const.tile([P, P], BF16)
        make_identity(nc, ident_bf16[:])

        w_words = const.tile([P, PASSES, 2 * CO], U8, align_bytes=64)
        w_scales = const.tile([P, PASSES, CO], U8, align_bytes=64)
        nc.vector.memset(w_scales[:].rearrange("p g n -> p (g n)").bitcast(I32), 0)

        shifted = [
            const.tile([P, PLANES, ROW], F32, name="shifted_even"),
            const.tile([P, PLANES, ROW], F32, name="shifted_odd"),
        ]
        for tile_ in shifted:
            nc.vector.memset(tile_[:, :, 0:PAD], 0.0)

        xv_bf16 = const.tile([P, PASSES, PACK], BF16)
        nc.scalar.dma_start(
            out=xv_bf16[:],
            in_=x_v[0][0].rearrange("(g p t) -> p g t", g=PASSES, p=P, t=PACK),
        )
        w_prev = const.tile([P, PLANES], F32)
        w_here = const.tile([P, PLANES], F32)
        v2_sb = const.tile([P, CO], BF16)
        v0_bf16 = const.tile([P, CO // P], BF16)
        v0_cols = const.tile([P, CO // P, P], F32)

        warm = const.tile([P, 2], F32)
        nc.vector.memset(warm[:], 0.0)
        nc.scalar.activation(out=warm[:, 1:2], in_=warm[:, 0:1], func=FUNC.Sigmoid)

        with nc.allow_non_contiguous_dma(reason="256 values, one to a partition and half"):
            nc.scalar.dma_start(out=v0_bf16[:], in_=v0[0][0].rearrange("(n c) -> c n", c=P))

        x_in, vh_in, vf_in = {}, {}, {}
        turned, planes, grouped_in, codes_of, scales_of = {}, {}, {}, {}, {}
        hidden_ps, hidden, z_acc, mix_of, v_acc, diff_of, step_of = {}, {}, {}, {}, {}, {}, {}
        result = {}

        def live(block):
            return 0 <= block < BLOCKS

        def place(block):
            return divmod(block * BLOCK, T)

        def load_x(block, x_tile, g0, g1, tiles=TILES):
            b, first = place(block)
            cols = slice(g0 * P * PACK, g1 * P * PACK)
            for j in range(0, TILES, tiles):
                rows = slice(first + j * P, first + (j + tiles) * P)
                nc.sync.dma_start(
                    out=x_tile[:, j : j + tiles, :],
                    in_=x[b, rows, cols].rearrange("(j p) k -> p j k", p=P),
                )
            for g in range(g0, g1):
                x_in[(block, g)] = x_tile[:, :, (g - g0) * P * PACK : (g - g0 + 1) * P * PACK]

        def load_x_block(block):
            if not live(block):
                return
            x_tile = loads.tile([P, TILES, C], BF16, name="x_sb", bufs=4)
            load_x(block, x_tile, 0, PASSES)

        def load_hidden(block):
            if not live(block):
                return
            b, first = place(block)
            vh_in[block] = loads.tile([P, TILES, DV], BF16, name="vh_sb", bufs=3)
            nc.sync.dma_start(
                out=vh_in[block][:],
                in_=v_hid[b, first : first + BLOCK, :].rearrange("(j p) k -> p j k", p=P),
            )

        def load_first(block):
            b, first = place(block)
            if not live(block) or first > 0:
                return
            vf_in[b] = loads.tile([P, T // P, CO], BF16, name="vf_sb", bufs=3)
            nc.sync.dma_start(out=vf_in[b][:], in_=v_first[b].rearrange("(j p) n -> p j n", p=P))

        def turn_part(block, bank, j0, j1, pool, name):
            g, u = divmod(bank, 2)
            xt = pool.tile([P, (j1 - j0) * P], F32, name=name)
            for j in range(j0, j1):
                words = x_in[(block, g)][:, j, :].bitcast(F32)
                nc.tensor.transpose(
                    xt[:, (j - j0) * P : (j - j0 + 1) * P], words[:, u::2], ident_f32[:]
                )
            turned.setdefault((block, bank), []).append((xt, j0 * P, j1 * P))

        def turn(block, bank):
            if not live(block):
                return
            turn_part(block, bank, 0, TILES, psum_x, "xt")

        def scale_prev(block, bank):
            if not live(block):
                return
            b, first = place(block)
            for xt, c0, c1 in turned[(block, bank)]:
                halves = xt[:].bitcast(BF16)
                for e in range(2):
                    plane = 2 * bank + e
                    nc.scalar.activation(
                        out=shifted[b % 2][:, plane, PAD + first + c0 : PAD + first + c1],
                        in_=halves[:, e : 2 * (c1 - c0) : 2],
                        func=FUNC.Copy,
                        scale=w_prev[:, plane : plane + 1],
                    )

        def mix_tokens(block, bank, which=(0, 1)):
            if not live(block):
                return
            b, first = place(block)
            if block not in planes:
                planes[block] = stage.tile([P, PLANES, BLOCK], BF16, name="xv_planes", bufs=3)
            for xt, c0, c1 in turned[(block, bank)]:
                halves = xt[:].bitcast(BF16)
                for e in which:
                    plane = 2 * bank + e
                    nc.vector.scalar_tensor_tensor(
                        out=planes[block][:, plane, c0:c1],
                        in0=halves[:, e : 2 * (c1 - c0) : 2],
                        scalar=w_here[:, plane : plane + 1],
                        in1=shifted[b % 2][:, plane, PAD - 1 + first + c0 : PAD - 1 + first + c1],
                        op0=ALU.mult,
                        op1=ALU.add,
                    )

        def gpsimd_tokens(block, g):
            return BLOCK if block == 0 else GPSIMD_TOKENS[g]

        def regroup_on_gpsimd(block, g):
            if not live(block):
                return
            if g == 0:
                grouped_in[block] = stage.tile(
                    [P, PASSES, BLOCK, PACK], BF16, name="grouped", bufs=1, align_bytes=64
                )
            nc.gpsimd.tensor_scalar(
                out=grouped_in[block][:, g, 0 : gpsimd_tokens(block, g), :],
                in0=planes[block][:, PACK * g : PACK * (g + 1), 0 : gpsimd_tokens(block, g)].rearrange(
                    "p t c -> p c t"
                ),
                scalar1=1.0,
                scalar2=0.0,
                op0=ALU.mult,
                op1=ALU.add,
            )

        def regroup_views(block, g, c0, c1):
            return (
                grouped_in[block][:, g, c0:c1, :].rearrange("p (c i) t -> p c t i", i=RUN),
                planes[block][:, PACK * g : PACK * (g + 1), c0:c1].rearrange(
                    "p t (c i) -> p c t i", i=RUN
                ),
            )

        def regroup_on_scalar(block, g):
            if not live(block) or gpsimd_tokens(block, g) == BLOCK:
                return
            grouped, flat = regroup_views(block, g, gpsimd_tokens(block, g), BLOCK)
            nc.scalar.copy(out=grouped, in_=flat)

        def quantise(block):
            if not live(block):
                return
            codes_of[block] = stage.tile([P, PASSES * BLOCK], U32, name="codes", bufs=3, align_bytes=64)
            scales_of[block] = stage.tile([P, PASSES * BLOCK], U8, name="scales", bufs=3, align_bytes=64)
            nc.vector.quantize_mx(
                out=codes_of[block][:].bitcast(FP8X4),
                scales=scales_of[block][:],
                in_=grouped_in[block][:].rearrange("p g c t -> p (g c t)"),
            )

        def project(block):
            if not live(block):
                return
            for pair in range(TILES // PAIR):
                if block == BLOCKS - 1:
                    v_ps = psum_x.tile([P, PAIR, CO], F32, name="xt")
                else:
                    v_ps = psum_v.tile([P, PAIR, CO], F32, name="v_ps")
                for i in range(PAIR):
                    j = pair * PAIR + i
                    for n in range(CO // P):
                        for g in range(PASSES):
                            cols = slice(g * BLOCK + j * P, g * BLOCK + (j + 1) * P)
                            nc.tensor.matmul_mx(
                                out=v_ps[:, i, n * P : (n + 1) * P],
                                lhsT=codes_of[block][:, cols].bitcast(FP8X4),
                                lhsT_scale=scales_of[block][:, cols],
                                rhs=w_words[:, g, 2 * P * n : 2 * P * (n + 1)].bitcast(FP4X4),
                                rhs_scale=w_scales[:, g, n * P : (n + 1) * P],
                                start=(g == 0),
                                stop=(g == PASSES - 1),
                            )
                v_acc[(block, pair)] = v_ps

        def turn_hidden(block):
            if not live(block):
                return
            hidden_ps[block] = psum_h.tile([P, BLOCK], BF16, name="vht_ps")
            for j in range(TILES):
                nc.tensor.transpose(
                    hidden_ps[block][:, j * P : (j + 1) * P], vh_in[block][:, j, :], ident_bf16[:]
                )

        def copy_hidden(block):
            if not live(block):
                return
            hidden[block] = stage.tile([P, BLOCK], BF16, name="vht")
            nc.scalar.copy(out=hidden[block][:], in_=hidden_ps[block][:])

        def gate(block, pair):
            if not live(block):
                return
            z_ps = psum_z.tile([P, PAIR, CO], F32, name="z_ps")
            for i in range(PAIR):
                j = pair * PAIR + i
                for n in range(CO // P):
                    nc.tensor.matmul(
                        out=z_ps[:, i, n * P : (n + 1) * P],
                        lhsT=v0_cols[:, n, :],
                        rhs=ident_f32[:],
                        is_transpose=True,
                        start=(n == 0),
                        stop=False,
                    )
                nc.tensor.matmul(
                    out=z_ps[:, i, :],
                    lhsT=hidden[block][:, j * P : (j + 1) * P],
                    rhs=v2_sb[:],
                    start=False,
                    stop=True,
                )
            z_acc[(block, pair)] = z_ps

        def squash(block, pair):
            if not live(block):
                return
            mix_of[(block, pair)] = blend.tile([P, PAIR, CO], F32, name="mix", bufs=4)
            nc.scalar.activation(
                out=mix_of[(block, pair)][:], in_=z_acc[(block, pair)][:], func=FUNC.Sigmoid
            )

        def difference(block, pair):
            if not live(block):
                return
            b, first = place(block)
            j = first // P + pair * PAIR
            diff_of[(block, pair)] = blend.tile([P, PAIR, CO], F32, name="diff")
            nc.vector.tensor_tensor(
                out=diff_of[(block, pair)][:],
                in0=vf_in[b][:, j : j + PAIR, :],
                in1=v_acc[(block, pair)][:],
                op=ALU.subtract,
            )

        def product(block, pair, engine=nc.gpsimd):
            if not live(block):
                return
            step_of[(block, pair)] = blend.tile([P, PAIR, CO], F32, name="step")
            engine.tensor_tensor(
                out=step_of[(block, pair)][:],
                in0=diff_of[(block, pair)][:],
                in1=mix_of[(block, pair)][:],
                op=ALU.mult,
            )

        def blend_finish(block, pair):
            if not live(block):
                return
            b, first = place(block)
            if pair == 0:
                result[block] = blend.tile([P, TILES, CO], F32, name="res", bufs=10)
            tiles = slice(pair * PAIR, (pair + 1) * PAIR)
            nc.vector.tensor_tensor(
                out=result[block][:, tiles, :],
                in0=step_of[(block, pair)][:],
                in1=v_acc[(block, pair)][:],
                op=ALU.add,
            )
            if block == BLOCKS - 1:
                store(block, tiles)
            elif pair == TILES // PAIR - 1:
                store(block, slice(0, TILES))

        def store(block, tiles):
            b, first = place(block)
            rows = slice(first + tiles.start * P, first + tiles.stop * P)
            nc.sync.dma_start(
                out=out[b, rows, :].rearrange("(j p) n -> p j n", p=P), in_=result[block][:, tiles, :]
            )

        for g in range(PASSES):
            x_pass = const.tile([P, TILES, P * PACK], BF16, name="x_pass%d" % g)
            load_x(0, x_pass, g, g + 1, tiles=1 if g == 0 else TILES)
        load_hidden(0)
        load_x_block(1)
        nc.sync.dma_start(out=v2_sb[:], in_=v2)
        load_hidden(1)
        load_x_block(2)
        nc.sync.dma_start(
            out=w_words[:].bitcast(I32), in_=W_v_words.bitcast(I32).rearrange("g p n -> p g n")
        )
        for quad in range(4):
            nc.sync.dma_start(
                out=w_scales[32 * quad : 32 * quad + 4, :, :].bitcast(I32),
                in_=W_v_scales[:, 4 * quad : 4 * quad + 4, :]
                .bitcast(I32)
                .rearrange("g r n -> r g n"),
            )
        load_first(0)

        nc.vector.tensor_copy(out=w_prev[:], in_=xv_bf16[:].rearrange("p g t -> p (g t)"))
        nc.vector.tensor_scalar(
            out=w_here[:], in0=w_prev[:], scalar1=-1.0, scalar2=1.0, op0=ALU.mult, op1=ALU.add
        )
        nc.gpsimd.tensor_copy(
            out=v0_cols[:], in_=v0_bf16[:].unsqueeze(2).to_broadcast([P, CO // P, P])
        )

        turn_part(0, 0, 0, 1, psum_v, "v_ps")
        turn_part(0, 0, 1, 2, psum_v, "v_ps")
        turn_part(0, 0, 2, TILES, psum_x, "xt")
        turn(0, 1)
        turn(0, 2)
        scale_prev(0, 0)
        turn(0, 3)
        mix_tokens(0, 0)
        turned[(0, 0)] = []

        for i in range(BLOCKS - 1):
            load_x_block(i + 3)
            load_hidden(i + 2)
            load_first(i + 2)

            scale_prev(i, 1)
            regroup_on_scalar(i - 1, 1)
            mix_tokens(i, 0, (0,))
            difference(i - 2, 0)
            mix_tokens(i, 0, (1,))
            regroup_on_gpsimd(i - 1, 1)
            product(i - 2, 0)
            difference(i - 2, 1)
            product(i - 2, 1)
            turn_hidden(i)
            turn(i + 1, 0)

            scale_prev(i, 2)
            squash(i - 1, 0)
            mix_tokens(i, 1)
            turn(i + 1, 1)

            scale_prev(i, 3)
            copy_hidden(i)
            mix_tokens(i, 2)
            quantise(i - 1)
            blend_finish(i - 2, 0)
            blend_finish(i - 2, 1)
            regroup_on_gpsimd(i, 0)
            gate(i - 1, 1)
            turn(i + 1, 2)

            scale_prev(i + 1, 0)
            regroup_on_scalar(i, 0)
            squash(i - 1, 1)
            mix_tokens(i, 3)
            project(i - 1)
            gate(i, 0)
            turn(i + 1, 3)

        last = BLOCKS - 1
        scale_prev(last, 1)
        regroup_on_scalar(last - 1, 1)
        mix_tokens(last, 0, (0,))
        difference(last - 2, 0)
        mix_tokens(last, 0, (1,))
        regroup_on_gpsimd(last - 1, 1)
        product(last - 2, 0)
        difference(last - 2, 1)
        product(last - 2, 1)
        turn_hidden(last)

        scale_prev(last, 2)
        squash(last - 1, 0)
        mix_tokens(last, 1)

        scale_prev(last, 3)
        copy_hidden(last)
        mix_tokens(last, 2)
        quantise(last - 1)
        blend_finish(last - 2, 0)
        blend_finish(last - 2, 1)
        regroup_on_gpsimd(last, 0)
        gate(last - 1, 1)

        squash(last - 1, 1)
        regroup_on_scalar(last, 0)
        mix_tokens(last, 3)
        gate(last, 0)
        project(last - 1)
        squash(last, 0)
        gate(last, 1)

        grouped, flat = regroup_views(last, PASSES - 1, LAST_GPSIMD_TOKENS, BLOCK)
        nc.scalar.copy(out=grouped, in_=flat)
        nc.gpsimd.tensor_scalar(
            out=grouped_in[last][:, PASSES - 1, 0:LAST_GPSIMD_TOKENS, :],
            in0=planes[last][:, PACK * (PASSES - 1) :, 0:LAST_GPSIMD_TOKENS].rearrange("p t c -> p c t"),
            scalar1=1.0,
            scalar2=0.0,
            op0=ALU.mult,
            op1=ALU.add,
        )
        difference(last - 1, 0)
        difference(last - 1, 1)
        squash(last, 1)
        quantise(last)
        project(last)
        product(last - 1, 0, nc.vector)
        product(last - 1, 1)
        blend_finish(last - 1, 0)
        difference(last, 0)
        blend_finish(last - 1, 1)
        difference(last, 1)
        product(last, 0)
        product(last, 1, nc.vector)
        blend_finish(last, 0)
        blend_finish(last, 1)
